import numpy as np
import ml_dtypes


def mxq(x, axis, fmt="e4m3"):
    dtype, down = {"e4m3": (ml_dtypes.float8_e4m3fn, 7), "e5m2": (ml_dtypes.float8_e5m2, 14)}[fmt]
    v = np.moveaxis(np.asarray(x, np.float32).astype(ml_dtypes.bfloat16).astype(np.float64), axis, -1)
    blocks = v.reshape(v.shape[:-1] + (-1, 32))
    amax = np.abs(blocks).max(-1, keepdims=True)
    byte = np.maximum(np.where(amax > 0, np.frexp(amax)[1] - 1 + 127, 0) - down, 1)
    scale = np.exp2(byte - 127.0)
    codes = (blocks / scale).astype(np.float32).astype(dtype).astype(np.float64)
    return np.moveaxis((codes * scale).reshape(v.shape), -1, axis)


WIDE = False


def mx_kscale(k):
    if not WIDE:
        return np.ones(k)
    levels = np.array([10, -10, 5, -5, 0])
    if k % 512:
        return np.exp2(np.random.permutation(np.resize(levels, k // 32))).repeat(32)
    a = np.empty((k // 512, 16))
    for p in range(k // 512):
        a[p, :8] = np.random.permutation(np.resize(levels, 8))
        for g in range(8):
            far = levels[np.abs(levels - a[p, g]) >= 10]
            a[p, g + 8] = far[np.random.randint(len(far))]
    return np.exp2(a.ravel()).repeat(32)


BF16 = ml_dtypes.bfloat16


def bf(x):
    return np.asarray(x, np.float32).astype(BF16)


def f64(x):
    return np.asarray(x).astype(np.float64)


B, T, HS, WS, C, HN, D = 1, 8, 8, 8, 3072, 24, 128
N = T * HS * WS
E = HN * D
EPS = 1e-6
BASE = 10000.0


def axis_angles(n, dim):
    f = 1.0 / BASE ** (np.arange(0, dim, 2)[: dim // 2] / dim)
    return np.repeat(np.arange(n)[:, None] * f[None, :], 2, axis=-1)


def rope_angles():
    dim_t = D - 4 * (D // 6)
    dim_h = 2 * (D // 6)
    dim_w = 2 * (D // 6)
    at = np.broadcast_to(axis_angles(T, dim_t)[:, None, None, :], (T, HS, WS, dim_t))
    ah = np.broadcast_to(axis_angles(HS, dim_h)[None, :, None, :], (T, HS, WS, dim_h))
    aw = np.broadcast_to(axis_angles(WS, dim_w)[None, None, :, :], (T, HS, WS, dim_w))
    return np.concatenate([at, ah, aw], axis=-1).reshape(N, D)


def rotate_half(v):
    p = v.reshape(v.shape[:-1] + (v.shape[-1] // 2, 2))
    return np.stack((-p[..., 1], p[..., 0]), axis=-1).reshape(v.shape)


def draw0():
    s = mx_kscale(C)
    return {"x": bf(np.random.standard_normal((B, N, C)) * s),
            "w": bf(np.random.standard_normal((E, C)) / np.sqrt(C) / s[None, :]),
            "b": bf(np.random.standard_normal(E) * 0.3),
            "norm_w": bf(1.0 + 0.1 * np.random.standard_normal(D))}


def core(x, w, b, norm_w):
    y = (mxq(f64(x), 2, "e4m3") @ mxq(f64(w), 1, "e4m3").T) + f64(b)
    y = y.reshape(B, N, HN, D).transpose(0, 2, 1, 3)
    u = y / np.sqrt(np.mean(y * y, axis=-1, keepdims=True) + EPS) * f64(norm_w)
    a = rope_angles()
    return u * np.cos(a) + rotate_half(u) * np.sin(a)


def e4m3fn_bytes(y):
    return np.clip(np.asarray(y, np.float64), -448.0, 448.0).astype(np.float32).astype(ml_dtypes.float8_e4m3fn).view(np.uint8)


def e4m3fn_values(b):
    return np.asarray(b, np.uint8).view(ml_dtypes.float8_e4m3fn).astype(np.float64)


def setup_inputs():
    d = draw0()
    x0 = np.asarray(d['w']).astype(np.float64)
    s = (np.max(np.abs(x0), axis=(0,), keepdims=True) / 448.0).astype(np.float32)
    out = {}
    for k, v in d.items():
        if k == 'w':
            out['w_bytes'] = e4m3fn_bytes(x0 / s.astype(np.float64))
            out['w_scale'] = s
        else:
            out[k] = v
    return out


def reference(x, w_bytes, w_scale, b, norm_w):
    return core(x, e4m3fn_values(w_bytes) * w_scale.astype(np.float64), b, norm_w)

@@ -1,0 +1,364 @@
+from contextlib import ExitStack
+
+import concourse.mybir as mybir
+from concourse.masks import make_identity
+
+F32 = mybir.dt.float32
+BF16 = mybir.dt.bfloat16
+I32 = mybir.dt.int32
+U32 = mybir.dt.uint32
+U8 = mybir.dt.uint8
+FP8 = mybir.dt.float8_e4m3fn
+FP8X4 = mybir.dt.float8_e4m3fn_x4
+ALU = mybir.AluOpType
+ACT = mybir.ActivationFunctionType
+
+P = 128
+TOKENS = 512
+K = 3072
+HEADS = 24
+PASSES = K // 512
+EPS = 1e-6
+PI = 3.141592653589793
+ONES_W = 64
+
+LAG_B, LAG_C, LAG_D, LAG_E, LAG_F = 1, 1, 2, 3, 4
+
+FLOPS = 2 * TOKENS * K * K
+
+
+def tile_attention_pa_kernel(tc, x, w_bytes, w_scale, b, norm_w, out):
+    nc = tc.nc
+    with ExitStack() as ctx:
+        const = ctx.enter_context(tc.tile_pool(name="const", bufs=1))
+        byte_pool = ctx.enter_context(tc.tile_pool(name="byte_pool", bufs=HEADS))
+        x_pool = ctx.enter_context(tc.tile_pool(name="x_pool", bufs=3))
+        xg_pool = ctx.enter_context(tc.tile_pool(name="xg_pool", bufs=4))
+        wb_pool = ctx.enter_context(tc.tile_pool(name="wb_pool", bufs=3))
+        grp_pool = ctx.enter_context(tc.tile_pool(name="grp_pool", bufs=3))
+        code_pool = ctx.enter_context(tc.tile_pool(name="code_pool", bufs=3))
+        epi_pool = ctx.enter_context(tc.tile_pool(name="epi_pool", bufs=3))
+        res_pool = ctx.enter_context(tc.tile_pool(name="res_pool", bufs=3))
+        psum_tp = ctx.enter_context(tc.psum_pool(name="psum_tp", bufs=4))
+        psum_z = ctx.enter_context(tc.psum_pool(name="psum_z", bufs=2))
+        psum_rot = ctx.enter_context(tc.psum_pool(name="psum_rot", bufs=1))
+        psum_ss = ctx.enter_context(tc.psum_pool(name="psum_ss", bufs=1))
+        ctx.enter_context(tc.manual_schedule())
+
+        scale_in = const.tile([P, P], F32, name="scale_in")
+        nc.gpsimd.memset(scale_in[32:64, :], 0.0)
+        nc.gpsimd.memset(scale_in[64:128, :], 0.0)
+        ident = const.tile([P, P], F32, name="ident")
+        make_identity(nc, ident[:])
+        d_int = const.tile([P, 1], I32, name="d_int")
+        nc.gpsimd.iota(d_int[:], pattern=[[0, 1]], base=0, channel_multiplier=1)
+        pos16 = const.tile([P, 16], F32, name="pos16")
+        nc.gpsimd.iota(pos16[:], pattern=[[0, 2], [1, 8]], base=0, channel_multiplier=0, allow_small_or_imprecise_dtypes=True)
+        base_col = const.tile([P, 1], F32, name="base_col")
+        nc.gpsimd.memset(base_col[:], 10000.0)
+        vec_rows = const.tile([P, P], BF16, name="vec_rows")
+        nc.gpsimd.memset(vec_rows[:], 0.0)
+
+        scale_view = w_scale.rearrange("o (m q) -> (o m) q", q=P)
+        nc.sync.dma_start(out=scale_in[0:HEADS, :], in_=scale_view)
+        nc.sync.dma_start(out=scale_in[HEADS:32, :], in_=scale_view[0 : 32 - HEADS, :])
+        w_rows = []
+
+        def load_w(h):
+            t = byte_pool.tile([P, K], U8, name="w_code_bytes", tag="w_code_bytes")
+            nc.sync.dma_start(out=t[:], in_=w_bytes[h * P : (h + 1) * P, :])
+            w_rows.append(t)
+
+        x_view = x[0].rearrange("(j p) k -> p j k", p=P)
+        x_parts = []
+
+        def load_x(c):
+            t = x_pool.tile([P, 4, 1024], BF16, name="x_part", tag="x_part")
+            nc.sync.dma_start(out=t[:], in_=x_view[:, :, c * 1024 : (c + 1) * 1024])
+            x_parts.append(t)
+
+        load_w(0)
+        load_x(0)
+        load_w(1)
+        nc.sync.dma_start(out=vec_rows[0:HEADS, :], in_=b.rearrange("(h d) -> h d", d=P))
+        nc.sync.dma_start(out=vec_rows[HEADS : HEADS + 1, :], in_=norm_w.rearrange("(o d) -> o d", o=1))
+        load_x(1)
+        load_x(2)
+        for h in range(2, HEADS):
+            load_w(h)
+
+        scale_rows = const.tile([P, K], F32, name="scale_rows")
+        odd_int = const.tile([P, 1], I32, name="odd_int")
+        nc.vector.tensor_scalar(out=odd_int[:], in0=d_int[:], scalar1=1, scalar2=None, op0=ALU.bitwise_and)
+        d_col = const.tile([P, 1], F32, name="d_col")
+        nc.vector.tensor_copy(out=d_col[:], in_=d_int[:])
+        odd = const.tile([P, 1], F32, name="odd")
+        nc.vector.tensor_copy(out=odd[:], in_=odd_int[:])
+        is_h = const.tile([P, 1], F32, name="is_h")
+        nc.vector.tensor_scalar(out=is_h[:], in0=d_col[:], scalar1=44.0, scalar2=None, op0=ALU.is_ge)
+        is_w = const.tile([P, 1], F32, name="is_w")
+        nc.vector.tensor_scalar(out=is_w[:], in0=d_col[:], scalar1=86.0, scalar2=None, op0=ALU.is_ge)
+        even_d = const.tile([P, 1], F32, name="even_d")
+        nc.vector.tensor_tensor(out=even_d[:], in0=d_col[:], in1=odd[:], op=ALU.subtract)
+        m2a = const.tile([P, 1], F32, name="m2a")
+        nc.vector.scalar_tensor_tensor(out=m2a[:], in0=is_h[:], scalar=-44.0, in1=even_d[:], op0=ALU.mult, op1=ALU.add)
+        m2 = const.tile([P, 1], F32, name="m2")
+        nc.vector.scalar_tensor_tensor(out=m2[:], in0=is_w[:], scalar=-42.0, in1=m2a[:], op0=ALU.mult, op1=ALU.add)
+        neg_inv_dim = const.tile([P, 1], F32, name="neg_inv_dim")
+        nc.vector.tensor_scalar(out=neg_inv_dim[:], in0=is_h[:], scalar1=1.0 / 44.0 - 1.0 / 42.0, scalar2=-1.0 / 44.0, op0=ALU.mult, op1=ALU.add)
+        expo = const.tile([P, 1], F32, name="expo")
+        nc.vector.tensor_tensor(out=expo[:], in0=m2[:], in1=neg_inv_dim[:], op=ALU.mult)
+        freq = const.tile([P, 1], F32, name="freq")
+        nc.gpsimd.tensor_tensor(out=freq[:], in0=base_col[:], in1=expo[:], op=ALU.pow)
+        sign = const.tile([P, 1], F32, name="sign")
+        nc.vector.tensor_scalar(out=sign[:], in0=odd[:], scalar1=-2.0, scalar2=1.0, op0=ALU.mult, op1=ALU.add)
+        mask_t = const.tile([P, 1], F32, name="mask_t")
+        nc.vector.tensor_scalar(out=mask_t[:], in0=is_h[:], scalar1=-1.0, scalar2=1.0, op0=ALU.mult, op1=ALU.add)
+        mask_h = const.tile([P, 1], F32, name="mask_h")
+        nc.vector.tensor_tensor(out=mask_h[:], in0=is_h[:], in1=is_w[:], op=ALU.subtract)
+
+        ident_bf = const.tile([P, P], BF16, name="ident_bf")
+        make_identity(nc, ident_bf[:])
+        swap = const.tile([P, P], F32, name="swap")
+        ident_pairs = ident[:].rearrange("p (m e) -> p m e", e=2)
+        swap_pairs = swap[:].rearrange("p (m e) -> p m e", e=2)
+        nc.gpsimd.tensor_copy(out=swap_pairs[:, :, 0], in_=ident_pairs[:, :, 1])
+        nc.gpsimd.tensor_copy(out=swap_pairs[:, :, 1], in_=ident_pairs[:, :, 0])
+        ones = const.tile([P, ONES_W], F32, name="ones")
+        nc.gpsimd.memset(ones[:], 1.0)
+        eps_col = const.tile([P, 1], F32, name="eps_col")
+        nc.gpsimd.memset(eps_col[:], EPS)
+
+        sin_cos = const.tile([P, 16], F32, name="sin_cos")
+        vec_cols = const.tile([P, 32], F32, name="vec_cols")
+        vec_scaled = const.tile([P, 32], F32, name="vec_scaled")
+        tables = const.tile([P, 2, TOKENS], F32, name="tables")
+
+        def spread_scales():
+            turned = psum_tp.tile([P, P], F32, name="turned", tag="tp")
+            nc.tensor.transpose(turned[:], scale_in[:], ident[:])
+            scale_cols = const.tile([P, HEADS], F32, name="scale_cols")
+            nc.scalar.copy(out=scale_cols[:], in_=turned[:, 0:HEADS])
+            for c in range(PASSES):
+                spread = psum_tp.tile([P, 4, P], F32, name="spread", tag="tp")
+                for a in range(4):
+                    m = 4 * c + a
+                    nc.tensor.transpose(spread[:, a, :], scale_cols[:, m : m + 1].to_broadcast([P, P]), ident[:])
+                nc.scalar.copy(out=scale_rows[:, c * 512 : (c + 1) * 512], in_=spread[:].rearrange("p a q -> p (a q)"))
+
+        def angles():
+            angle = const.tile([P, 16], F32, name="angle")
+            nc.vector.tensor_scalar(out=angle[:], in0=pos16[:], scalar1=freq[:, 0:1], scalar2=None, op0=ALU.mult)
+            nc.vector.tensor_scalar(out=angle[:, 0:8], in0=angle[:, 0:8], scalar1=PI / 2.0, scalar2=None, op0=ALU.add)
+            wrap = const.tile([P, 16], F32, name="wrap")
+            nc.vector.tensor_scalar(out=wrap[:], in0=angle[:], scalar1=PI, scalar2=-2.0 * PI, op0=ALU.is_gt, op1=ALU.mult)
+            folded = const.tile([P, 16], F32, name="folded")
+            nc.vector.tensor_tensor(out=folded[:], in0=angle[:], in1=wrap[:], op=ALU.add)
+            return folded
+
+        small_tabs = {}
+
+        def turn_vectors():
+            vec_ps = psum_tp.tile([P, P], BF16, name="vec_ps", tag="tp")
+            nc.tensor.transpose(vec_ps[:], vec_rows[:], ident_bf[:])
+            nc.scalar.copy(out=vec_cols[:], in_=vec_ps[:, 0:32])
+            nc.scalar.activation(out=vec_scaled[:], in_=vec_cols[:], func=ACT.Copy, scale=float(P) ** -0.5)
+            gain = vec_cols[:, HEADS : HEADS + 1]
+            gain_signed = const.tile([P, 1], F32, name="gain_signed")
+            nc.scalar.activation(out=gain_signed[:], in_=sign[:], func=ACT.Copy, scale=gain)
+            tab = const.tile([P, 16], F32, name="tab")
+            nc.scalar.activation(out=tab[:, 0:8], in_=sin_cos[:, 0:8], func=ACT.Copy, scale=gain)
+            nc.scalar.activation(out=tab[:, 8:16], in_=sin_cos[:, 8:16], func=ACT.Copy, scale=gain_signed[:, 0:1])
+            for name, mask in (("t", mask_t), ("h", mask_h), ("w", is_w)):
+                masked = const.tile([P, 2, 8], F32, name="tab_" + name)
+                nc.scalar.activation(out=masked[:].rearrange("p w v -> p (w v)"), in_=tab[:], func=ACT.Copy, scale=mask[:, 0:1])
+                small_tabs[name] = masked
+
+        def build_tables():
+            by_ij = const.tile([P, 2, 64], F32, name="by_ij")
+            nc.vector.tensor_tensor(
+                out=by_ij[:].rearrange("p w (i j) -> p w i j", i=8),
+                in0=small_tabs["h"][:].unsqueeze(3).to_broadcast([P, 2, 8, 8]),
+                in1=small_tabs["w"][:].unsqueeze(2).to_broadcast([P, 2, 8, 8]),
+                op=ALU.add,
+            )
+            nc.vector.tensor_tensor(
+                out=tables[:].rearrange("p w (t r) -> p w t r", t=8),
+                in0=small_tabs["t"][:].unsqueeze(3).to_broadcast([P, 2, 8, 64]),
+                in1=by_ij[:].unsqueeze(2).to_broadcast([P, 2, 8, 64]),
+                op=ALU.add,
+            )
+
+        x_codes = const.tile([P, PASSES * TOKENS], U32, name="x_codes", align_bytes=64)
+        x_scales = const.tile([P, PASSES * TOKENS], U8, name="x_scales", align_bytes=64)
+        live = {}
+
+        def turn(dst_words, sources):
+            tp = psum_tp.tile([P, 2, 2, P], F32, name="tp", tag="tp")
+            for a in range(2):
+                for u in range(2):
+                    nc.tensor.transpose(tp[:, a, u, :], sources[a][u], ident[:])
+            nc.scalar.copy(out=dst_words, in_=tp[:].rearrange("p a u r -> p a r u"))
+
+        def x_turn(g, jp):
+            if jp == 0:
+                live[("xg", g)] = xg_pool.tile([P, 2048], BF16, name="xg", tag="xg", align_bytes=64)
+            lo = 256 * (g % 2)
+            turn(
+                live[("xg", g)][:, jp * 1024 : (jp + 1) * 1024].bitcast(F32).rearrange("p (a r u) -> p a r u", a=2, r=P, u=2),
+                [[x_parts[g // 2][:, 2 * jp + a, :].bitcast(F32)[:, lo + u : lo + 256 : 2] for u in range(2)] for a in range(2)],
+            )
+
+        def x_quantize(g):
+            cols = slice(g * TOKENS, (g + 1) * TOKENS)
+            nc.vector.quantize_mx(out=x_codes[:, cols].bitcast(FP8X4), scales=x_scales[:, cols], in_=live[("xg", g)][:])
+
+        def product(h):
+            pieces = 6 if h == 0 else 1
+            step = K // pieces
+            wb = wb_pool.tile([P, K], BF16, name="wb", tag="wb")
+            live[("wb", h)] = wb
+            for c in range(pieces):
+                cols = slice(c * step, (c + 1) * step)
+                nc.vector.tensor_tensor(out=wb[:, cols], in0=w_rows[h][:, cols].bitcast(FP8), in1=scale_rows[:, cols], op=ALU.mult)
+
+        def w_turn(h, s):
+            if s == 0:
+                live[("grp", h)] = grp_pool.tile([P, K], BF16, name="grp", tag="grp", align_bytes=64)
+            grp_words = live[("grp", h)][:].bitcast(F32).rearrange("p (g r u) -> p g r u", g=PASSES, r=P, u=2)
+            words = live[("wb", h)][:].bitcast(F32)
+            turn(
+                grp_words[:, 2 * s : 2 * s + 2, :, :],
+                [[words[:, 256 * (2 * s + a) + u : 256 * (2 * s + a + 1) : 2] for u in range(2)] for a in range(2)],
+            )
+
+        def w_quantize(h, lo, hi):
+            if lo == 0:
+                live[("wc", h)] = code_pool.tile([P, PASSES * P], U32, name="w_codes", tag="w_codes", align_bytes=64)
+                live[("ws", h)] = code_pool.tile([P, PASSES * P], U8, name="w_scales", tag="w_scales", align_bytes=64)
+            nc.vector.quantize_mx(
+                out=live[("wc", h)][:, lo // 4 : hi // 4].bitcast(FP8X4),
+                scales=live[("ws", h)][:, lo // 4 : hi // 4],
+                in_=live[("grp", h)][:, lo:hi],
+            )
+
+        def multiply(h, s):
+            if s == 0:
+                live[("z", h)] = psum_z.tile([P, TOKENS], F32, name="z", tag="z")
+            for g in (2 * s, 2 * s + 1):
+                nc.tensor.matmul_mx(
+                    out=live[("z", h)][:],
+                    lhsT=live[("wc", h)][:, g * P : (g + 1) * P].bitcast(FP8X4),
+                    lhsT_scale=live[("ws", h)][:, g * P : (g + 1) * P],
+                    rhs=x_codes[:, g * TOKENS : (g + 1) * TOKENS].bitcast(FP8X4),
+                    rhs_scale=x_scales[:, g * TOKENS : (g + 1) * TOKENS],
+                    start=(g == 0),
+                    stop=(g == PASSES - 1),
+                )
+
+        def squares(h):
+            sq = epi_pool.tile([P, TOKENS], F32, name="sq", tag="sq")
+            live[("sq", h)] = sq
+            nc.scalar.activation(out=sq[:], in_=live[("z", h)][:], func=ACT.Square, bias=vec_scaled[:, h : h + 1], scale=float(P) ** -0.5)
+
+        def table_products(h):
+            prod = epi_pool.tile([P, 2, TOKENS], F32, name="prod", tag="prod")
+            live[("prod", h)] = prod
+            pieces = 2 if h == HEADS - 1 else 1
+            step = TOKENS // pieces
+            for c in range(pieces):
+                cols = slice(c * step, (c + 1) * step)
+                nc.vector.scalar_tensor_tensor(
+                    out=prod[:, :, cols],
+                    in0=live[("z", h)][:, cols].unsqueeze(1).to_broadcast([P, 2, step]),
+                    scalar=vec_cols[:, h : h + 1],
+                    in1=tables[:, :, cols],
+                    op0=ALU.add,
+                    op1=ALU.mult,
+                )
+
+        def turn_back(h, s):
+            if s == 0:
+                ss = psum_ss.tile([P, 4, ONES_W], F32, name="ss", tag="ss")
+                live[("ss", h)] = ss
+                for j in range(4):
+                    nc.tensor.matmul(ss[:, j, :], lhsT=live[("sq", h)][:, j * P : (j + 1) * P], rhs=ones[:], start=True, stop=True)
+                return
+            if s == 1:
+                live[("rot", h)] = psum_rot.tile([P, 4, P], F32, name="rot", tag="rot")
+            rot = live[("rot", h)]
+            for j in (2 * s - 2, 2 * s - 1):
+                cols = slice(j * P, (j + 1) * P)
+                nc.tensor.matmul(rot[:, j, :], lhsT=live[("prod", h)][:, 0, cols], rhs=ident[:], is_transpose=True, start=True, stop=False)
+                nc.tensor.matmul(rot[:, j, :], lhsT=live[("prod", h)][:, 1, cols], rhs=swap[:], is_transpose=True, start=False, stop=True)
+
+        def finish(h):
+            rstd = res_pool.tile([P, 4], F32, name="rstd", tag="rstd")
+            nc.scalar.activation(out=rstd[:], in_=live[("ss", h)][:, :, 0], func=ACT.Abs_reciprocal_sqrt, bias=eps_col[:, 0:1], scale=1.0)
+            res = res_pool.tile([P, 4, P], F32, name="res", tag="res")
+            out_view = out[0, h].rearrange("(j p) d -> p j d", p=P)
+            pieces = 2 if h == HEADS - 1 else 1
+            step = 4 // pieces
+            for c in range(pieces):
+                for j in range(c * step, (c + 1) * step):
+                    nc.scalar.activation(out=res[:, j, :], in_=live[("rot", h)][:, j, :], func=ACT.Copy, scale=rstd[:, j : j + 1])
+                nc.sync.dma_start(out=out_view[:, c * step : (c + 1) * step, :], in_=res[:, c * step : (c + 1) * step, :])
+
+        def on(h):
+            return 0 <= h < HEADS
+
+        x_turns = {(0, 0): (0,), (0, 1): (1,), (1, 0): (2,), (1, 1): (3,), (1, 2): (4, 5)}
+        x_quants = {0: (0, 1), 1: (2, 3, 4, 5)}
+
+        folded_angles = angles()
+        spread_scales()
+        nc.scalar.activation(out=sin_cos[:], in_=folded_angles[:], func=ACT.Sin)
+        for i in range(HEADS):
+            product(i)
+            if i == 2:
+                build_tables()
+            if on(i - LAG_E):
+                squares(i - LAG_E)
+            for s in range(3):
+                if on(i - LAG_B):
+                    w_turn(i - LAG_B, s)
+                for g in x_turns.get((i, s), ()):
+                    x_turn(g, 0)
+                    x_turn(g, 1)
+                if on(i - LAG_F):
+                    turn_back(i - LAG_F, s)
+                if on(i - LAG_D):
+                    multiply(i - LAG_D, s)
+                if s == 1:
+                    if on(i - LAG_C):
+                        w_quantize(i - LAG_C, 0, 2048)
+                    if on(i - LAG_E):
+                        table_products(i - LAG_E)
+            if on(i - LAG_C):
+                w_quantize(i - LAG_C, 2048, 3072)
+            for g in x_quants.get(i, ()):
+                x_quantize(g)
+            if on(i - LAG_F):
+                finish(i - LAG_F)
+            if i == 1:
+                turn_vectors()
+
+        last = HEADS - 1
+        squares(last - 2)
+        table_products(last - 2)
+        for s in range(3):
+            w_turn(last, s)
+        w_quantize(last, 0, 2048)
+        w_quantize(last, 2048, 3072)
+        for h in (last - 1, last):
+            for s in range(3):
+                turn_back(h - 2, s)
+            finish(h - 2)
+            for s in range(3):
+                multiply(h, s)
+            squares(h)
+            table_products(h)
+        for h in (last - 1, last):
+            for s in range(3):
+                turn_back(h, s)
+            finish(h)

@@ -45,19 +45,18 @@ def tile_attention_pa_kernel(tc, x, w_bytes, w_scale, b, norm_w, out):
         psum_ss = ctx.enter_context(tc.psum_pool(name="psum_ss", bufs=1))
         ctx.enter_context(tc.manual_schedule())
 
-        scale_in = const.tile([P, P], F32, name="scale_in")
-        nc.gpsimd.memset(scale_in[32:64, :], 0.0)
-        nc.gpsimd.memset(scale_in[64:128, :], 0.0)
-        ident = const.tile([P, P], F32, name="ident")
-        make_identity(nc, ident[:])
         d_int = const.tile([P, 1], I32, name="d_int")
         nc.gpsimd.iota(d_int[:], pattern=[[0, 1]], base=0, channel_multiplier=1)
-        pos16 = const.tile([P, 16], F32, name="pos16")
-        nc.gpsimd.iota(pos16[:], pattern=[[0, 2], [1, 8]], base=0, channel_multiplier=0, allow_small_or_imprecise_dtypes=True)
+        col_idx = const.tile([P, P], F32, name="col_idx")
+        nc.gpsimd.iota(col_idx[:], pattern=[[1, P]], base=0, channel_multiplier=0, allow_small_or_imprecise_dtypes=True)
+        scale_in = const.tile([P, P], F32, name="scale_in")
+        nc.vector.memset(scale_in[32:64, :], 0.0)
+        nc.vector.memset(scale_in[64:128, :], 0.0)
         base_col = const.tile([P, 1], F32, name="base_col")
-        nc.gpsimd.memset(base_col[:], 10000.0)
+        nc.vector.memset(base_col[:], 10000.0)
         vec_rows = const.tile([P, P], BF16, name="vec_rows")
-        nc.gpsimd.memset(vec_rows[:], 0.0)
+        nc.vector.memset(vec_rows[:], 0.0)
+        ident = const.tile([P, P], F32, name="ident")
 
         scale_view = w_scale.rearrange("o (m q) -> (o m) q", q=P)
         nc.sync.dma_start(out=scale_in[0:HEADS, :], in_=scale_view)
@@ -110,6 +109,7 @@ def tile_attention_pa_kernel(tc, x, w_bytes, w_scale, b, norm_w, out):
         nc.vector.tensor_tensor(out=expo[:], in0=m2[:], in1=neg_inv_dim[:], op=ALU.mult)
         freq = const.tile([P, 1], F32, name="freq")
         nc.gpsimd.tensor_tensor(out=freq[:], in0=base_col[:], in1=expo[:], op=ALU.pow)
+        nc.vector.tensor_scalar(out=ident[:], in0=col_idx[:], scalar1=d_col[:, 0:1], scalar2=None, op0=ALU.is_equal)
         sign = const.tile([P, 1], F32, name="sign")
         nc.vector.tensor_scalar(out=sign[:], in0=odd[:], scalar1=-2.0, scalar2=1.0, op0=ALU.mult, op1=ALU.add)
         mask_t = const.tile([P, 1], F32, name="mask_t")
@@ -133,6 +133,7 @@ def tile_attention_pa_kernel(tc, x, w_bytes, w_scale, b, norm_w, out):
         vec_cols = const.tile([P, 32], F32, name="vec_cols")
         vec_scaled = const.tile([P, 32], F32, name="vec_scaled")
         tables = const.tile([P, 2, TOKENS], F32, name="tables")
+        raw_tables = const.tile([P, 2, TOKENS], F32, name="raw_tables")
 
         def spread_scales():
             turned = psum_tp.tile([P, P], F32, name="turned", tag="tp")
@@ -148,12 +149,13 @@ def tile_attention_pa_kernel(tc, x, w_bytes, w_scale, b, norm_w, out):
 
         def angles():
             angle = const.tile([P, 16], F32, name="angle")
-            nc.vector.tensor_scalar(out=angle[:], in0=pos16[:], scalar1=freq[:, 0:1], scalar2=None, op0=ALU.mult)
-            nc.vector.tensor_scalar(out=angle[:, 0:8], in0=angle[:, 0:8], scalar1=PI / 2.0, scalar2=None, op0=ALU.add)
+            nc.vector.tensor_scalar(out=angle[:, 0:8], in0=col_idx[:, 0:8], scalar1=freq[:, 0:1], scalar2=PI / 2.0, op0=ALU.mult, op1=ALU.add)
+            nc.vector.tensor_scalar(out=angle[:, 8:16], in0=col_idx[:, 0:8], scalar1=freq[:, 0:1], scalar2=None, op0=ALU.mult)
             wrap = const.tile([P, 16], F32, name="wrap")
             nc.vector.tensor_scalar(out=wrap[:], in0=angle[:], scalar1=PI, scalar2=-2.0 * PI, op0=ALU.is_gt, op1=ALU.mult)
             folded = const.tile([P, 16], F32, name="folded")
             nc.vector.tensor_tensor(out=folded[:], in0=angle[:], in1=wrap[:], op=ALU.add)
+            nc.vector.tensor_scalar(out=folded[:, 8:16], in0=folded[:, 8:16], scalar1=sign[:, 0:1], scalar2=None, op0=ALU.mult)
             return folded
 
         small_tabs = {}
@@ -164,17 +166,15 @@ def tile_attention_pa_kernel(tc, x, w_bytes, w_scale, b, norm_w, out):
             nc.scalar.copy(out=vec_cols[:], in_=vec_ps[:, 0:32])
             nc.scalar.activation(out=vec_scaled[:], in_=vec_cols[:], func=ACT.Copy, scale=float(P) ** -0.5)
             gain = vec_cols[:, HEADS : HEADS + 1]
-            gain_signed = const.tile([P, 1], F32, name="gain_signed")
-            nc.scalar.activation(out=gain_signed[:], in_=sign[:], func=ACT.Copy, scale=gain)
-            tab = const.tile([P, 16], F32, name="tab")
-            nc.scalar.activation(out=tab[:, 0:8], in_=sin_cos[:, 0:8], func=ACT.Copy, scale=gain)
-            nc.scalar.activation(out=tab[:, 8:16], in_=sin_cos[:, 8:16], func=ACT.Copy, scale=gain_signed[:, 0:1])
-            for name, mask in (("t", mask_t), ("h", mask_h), ("w", is_w)):
-                masked = const.tile([P, 2, 8], F32, name="tab_" + name)
-                nc.scalar.activation(out=masked[:].rearrange("p w v -> p (w v)"), in_=tab[:], func=ACT.Copy, scale=mask[:, 0:1])
-                small_tabs[name] = masked
+            nc.scalar.activation(
+                out=tables[:].rearrange("p w n -> p (w n)"), in_=raw_tables[:].rearrange("p w n -> p (w n)"), func=ACT.Copy, scale=gain
+            )
 
         def build_tables():
+            for name, mask in (("t", mask_t), ("h", mask_h), ("w", is_w)):
+                masked = const.tile([P, 2, 8], F32, name="tab_" + name)
+                nc.vector.tensor_scalar(out=masked[:].rearrange("p w v -> p (w v)"), in0=sin_cos[:], scalar1=mask[:, 0:1], scalar2=None, op0=ALU.mult)
+                small_tabs[name] = masked
             by_ij = const.tile([P, 2, 64], F32, name="by_ij")
             nc.vector.tensor_tensor(
                 out=by_ij[:].rearrange("p w (i j) -> p w i j", i=8),
@@ -183,7 +183,7 @@ def tile_attention_pa_kernel(tc, x, w_bytes, w_scale, b, norm_w, out):
                 op=ALU.add,
             )
             nc.vector.tensor_tensor(
-                out=tables[:].rearrange("p w (t r) -> p w t r", t=8),
+                out=raw_tables[:].rearrange("p w (t r) -> p w t r", t=8),
                 in0=small_tabs["t"][:].unsqueeze(3).to_broadcast([P, 2, 8, 64]),
                 in1=by_ij[:].unsqueeze(2).to_broadcast([P, 2, 8, 64]),
                 op=ALU.add,
@@ -311,12 +311,11 @@ def tile_attention_pa_kernel(tc, x, w_bytes, w_scale, b, norm_w, out):
         x_quants = {0: (0, 1), 1: (2, 3, 4, 5)}
 
         folded_angles = angles()
-        spread_scales()
         nc.scalar.activation(out=sin_cos[:], in_=folded_angles[:], func=ACT.Sin)
+        build_tables()
+        spread_scales()
         for i in range(HEADS):
             product(i)
-            if i == 2:
-                build_tables()
             if on(i - LAG_E):
                 squares(i - LAG_E)
             for s in range(3):

@@ -307,8 +307,9 @@ def tile_attention_pa_kernel(tc, x, w_bytes, w_scale, b, norm_w, out):
         def on(h):
             return 0 <= h < HEADS
 
-        x_turns = {(0, 0): (0,), (0, 1): (1,), (1, 0): (2,), (1, 1): (3,), (1, 2): (4, 5)}
-        x_quants = {0: (0, 1), 1: (2, 3, 4, 5)}
+        x_turns = {(0, 0): (0,), (0, 1): (1,), (1, 2): (2, 3), (2, 0): (4,), (2, 1): (5,)}
+        x_quants_early = {1: (0, 1), 2: (2, 3)}
+        x_quants_late = {2: (4, 5)}
 
         folded_angles = angles()
         nc.scalar.activation(out=sin_cos[:], in_=folded_angles[:], func=ACT.Sin)
@@ -324,19 +325,21 @@ def tile_attention_pa_kernel(tc, x, w_bytes, w_scale, b, norm_w, out):
                 for g in x_turns.get((i, s), ()):
                     x_turn(g, 0)
                     x_turn(g, 1)
+                if s == 1:
+                    for g in x_quants_early.get(i, ()):
+                        x_quantize(g)
+                    if on(i - LAG_C):
+                        w_quantize(i - LAG_C, 0, 2048)
+                    for g in x_quants_late.get(i, ()):
+                        x_quantize(g)
+                    if on(i - LAG_E):
+                        table_products(i - LAG_E)
                 if on(i - LAG_F):
                     turn_back(i - LAG_F, s)
                 if on(i - LAG_D):
                     multiply(i - LAG_D, s)
-                if s == 1:
-                    if on(i - LAG_C):
-                        w_quantize(i - LAG_C, 0, 2048)
-                    if on(i - LAG_E):
-                        table_products(i - LAG_E)
             if on(i - LAG_C):
                 w_quantize(i - LAG_C, 2048, 3072)
-            for g in x_quants.get(i, ()):
-                x_quantize(g)
             if on(i - LAG_F):
                 finish(i - LAG_F)
             if i == 1:

@@ -242,10 +242,10 @@ def tile_attention_pa_kernel(tc, x, w_bytes, w_scale, b, norm_w, out):
                 in_=live[("grp", h)][:, lo:hi],
             )
 
-        def multiply(h, s):
-            if s == 0:
+        def multiply(h, passes):
+            if passes[0] == 0:
                 live[("z", h)] = psum_z.tile([P, TOKENS], F32, name="z", tag="z")
-            for g in (2 * s, 2 * s + 1):
+            for g in passes:
                 nc.tensor.matmul_mx(
                     out=live[("z", h)][:],
                     lhsT=live[("wc", h)][:, g * P : (g + 1) * P].bitcast(FP8X4),
@@ -277,17 +277,17 @@ def tile_attention_pa_kernel(tc, x, w_bytes, w_scale, b, norm_w, out):
                     op1=ALU.mult,
                 )
 
-        def turn_back(h, s):
-            if s == 0:
-                ss = psum_ss.tile([P, 4, ONES_W], F32, name="ss", tag="ss")
-                live[("ss", h)] = ss
-                for j in range(4):
-                    nc.tensor.matmul(ss[:, j, :], lhsT=live[("sq", h)][:, j * P : (j + 1) * P], rhs=ones[:], start=True, stop=True)
-                return
-            if s == 1:
+        def sums(h, tiles):
+            if tiles[0] == 0:
+                live[("ss", h)] = psum_ss.tile([P, 4, ONES_W], F32, name="ss", tag="ss")
+            for j in tiles:
+                nc.tensor.matmul(live[("ss", h)][:, j, :], lhsT=live[("sq", h)][:, j * P : (j + 1) * P], rhs=ones[:], start=True, stop=True)
+
+        def turn_back(h, tiles):
+            if tiles[0] == 0:
                 live[("rot", h)] = psum_rot.tile([P, 4, P], F32, name="rot", tag="rot")
             rot = live[("rot", h)]
-            for j in (2 * s - 2, 2 * s - 1):
+            for j in tiles:
                 cols = slice(j * P, (j + 1) * P)
                 nc.tensor.matmul(rot[:, j, :], lhsT=live[("prod", h)][:, 0, cols], rhs=ident[:], is_transpose=True, start=True, stop=False)
                 nc.tensor.matmul(rot[:, j, :], lhsT=live[("prod", h)][:, 1, cols], rhs=swap[:], is_transpose=True, start=False, stop=True)
@@ -319,25 +319,35 @@ def tile_attention_pa_kernel(tc, x, w_bytes, w_scale, b, norm_w, out):
             product(i)
             if on(i - LAG_E):
                 squares(i - LAG_E)
-            for s in range(3):
+            for s in range(2):
                 if on(i - LAG_B):
                     w_turn(i - LAG_B, s)
                 for g in x_turns.get((i, s), ()):
                     x_turn(g, 0)
                     x_turn(g, 1)
-                if s == 1:
-                    for g in x_quants_early.get(i, ()):
-                        x_quantize(g)
-                    if on(i - LAG_C):
-                        w_quantize(i - LAG_C, 0, 2048)
-                    for g in x_quants_late.get(i, ()):
-                        x_quantize(g)
-                    if on(i - LAG_E):
-                        table_products(i - LAG_E)
-                if on(i - LAG_F):
-                    turn_back(i - LAG_F, s)
-                if on(i - LAG_D):
-                    multiply(i - LAG_D, s)
+            for g in x_quants_early.get(i, ()):
+                x_quantize(g)
+            if on(i - LAG_C):
+                w_quantize(i - LAG_C, 0, 2048)
+            for g in x_quants_late.get(i, ()):
+                x_quantize(g)
+            if on(i - LAG_E):
+                table_products(i - LAG_E)
+            if on(i - LAG_F):
+                turn_back(i - LAG_F, (0, 1))
+                sums(i - LAG_F, (0, 1))
+            if on(i - LAG_D):
+                multiply(i - LAG_D, (0, 1, 2))
+            if on(i - LAG_B):
+                w_turn(i - LAG_B, 2)
+            for g in x_turns.get((i, 2), ()):
+                x_turn(g, 0)
+                x_turn(g, 1)
+            if on(i - LAG_F):
+                turn_back(i - LAG_F, (2, 3))
+                sums(i - LAG_F, (2, 3))
+            if on(i - LAG_D):
+                multiply(i - LAG_D, (3, 4, 5))
             if on(i - LAG_C):
                 w_quantize(i - LAG_C, 2048, 3072)
             if on(i - LAG_F):
@@ -353,14 +363,13 @@ def tile_attention_pa_kernel(tc, x, w_bytes, w_scale, b, norm_w, out):
         w_quantize(last, 0, 2048)
         w_quantize(last, 2048, 3072)
         for h in (last - 1, last):
-            for s in range(3):
-                turn_back(h - 2, s)
+            sums(h - 2, (0, 1, 2, 3))
+            turn_back(h - 2, (0, 1, 2, 3))
             finish(h - 2)
-            for s in range(3):
-                multiply(h, s)
+            multiply(h, (0, 1, 2, 3, 4, 5))
             squares(h)
             table_products(h)
         for h in (last - 1, last):
-            for s in range(3):
-                turn_back(h, s)
+            sums(h, (0, 1, 2, 3))
+            turn_back(h, (0, 1, 2, 3))
             finish(h)

@@ -23,6 +23,7 @@ PI = 3.141592653589793
 ONES_W = 64
 
 LAG_B, LAG_C, LAG_D, LAG_E, LAG_F = 1, 1, 2, 3, 4
+SCALAR_HEADS = tuple(range(1, HEADS, 2))
 
 FLOPS = 2 * TOKENS * K * K
 
@@ -61,6 +62,8 @@ def tile_attention_pa_kernel(tc, x, w_bytes, w_scale, b, norm_w, out):
         scale_view = w_scale.rearrange("o (m q) -> (o m) q", q=P)
         nc.sync.dma_start(out=scale_in[0:HEADS, :], in_=scale_view)
         nc.sync.dma_start(out=scale_in[HEADS:32, :], in_=scale_view[0 : 32 - HEADS, :])
+        scale_first = const.tile([P, 4], F32, name="scale_first")
+        nc.sync.dma_start(out=scale_first[:], in_=w_scale[:, 0:512].rearrange("o (p t) -> p (o t)", t=4))
         w_rows = []
 
         def load_w(h):
@@ -215,22 +218,36 @@ def tile_attention_pa_kernel(tc, x, w_bytes, w_scale, b, norm_w, out):
 
         def product(h):
             pieces = 6 if h == 0 else 1
-            step = K // pieces
+            first = 512 if h in SCALAR_HEADS else 0
+            step = (K - first) // pieces
             wb = wb_pool.tile([P, K], BF16, name="wb", tag="wb")
             live[("wb", h)] = wb
             for c in range(pieces):
-                cols = slice(c * step, (c + 1) * step)
+                cols = slice(first + c * step, first + (c + 1) * step)
                 nc.vector.tensor_tensor(out=wb[:, cols], in0=w_rows[h][:, cols].bitcast(FP8), in1=scale_rows[:, cols], op=ALU.mult)
+            if first:
+                nc.scalar.copy(out=wb[:, 0:first], in_=w_rows[h][:, 0:first].bitcast(FP8))
 
         def w_turn(h, s):
             if s == 0:
                 live[("grp", h)] = grp_pool.tile([P, K], BF16, name="grp", tag="grp", align_bytes=64)
             grp_words = live[("grp", h)][:].bitcast(F32).rearrange("p (g r u) -> p g r u", g=PASSES, r=P, u=2)
             words = live[("wb", h)][:].bitcast(F32)
-            turn(
-                grp_words[:, 2 * s : 2 * s + 2, :, :],
-                [[words[:, 256 * (2 * s + a) + u : 256 * (2 * s + a + 1) : 2] for u in range(2)] for a in range(2)],
-            )
+            sources = [[words[:, 256 * (2 * s + a) + u : 256 * (2 * s + a + 1) : 2] for u in range(2)] for a in range(2)]
+            if s == 0 and h in SCALAR_HEADS:
+                tp = psum_tp.tile([P, 2, 2, P], F32, name="tp", tag="tp")
+                for a in range(2):
+                    for u in range(2):
+                        nc.tensor.transpose(tp[:, a, u, :], sources[a][u], ident[:])
+                first = live[("grp", h)][:, 0:512].rearrange("p (r t) -> p r t", t=4)
+                for u in range(2):
+                    halves = tp[:, 0, u, :].bitcast(BF16).rearrange("p (r e) -> p r e", e=2)
+                    for e in range(2):
+                        t = 2 * u + e
+                        nc.scalar.activation(out=first[:, :, t], in_=halves[:, :, e], func=ACT.Copy, scale=scale_first[:, t : t + 1])
+                nc.scalar.copy(out=grp_words[:, 1, :, :], in_=tp[:, 1, :, :].rearrange("p u r -> p r u"))
+                return
+            turn(grp_words[:, 2 * s : 2 * s + 2, :, :], sources)
 
         def w_quantize(h, lo, hi):
             if lo == 0:

@@ -220,13 +220,16 @@ def tile_attention_pa_kernel(tc, x, w_bytes, w_scale, b, norm_w, out):
             pieces = 6 if h == 0 else 1
             first = 512 if h in SCALAR_HEADS else 0
             step = (K - first) // pieces
-            wb = wb_pool.tile([P, K], BF16, name="wb", tag="wb")
-            live[("wb", h)] = wb
+            if not first:
+                live[("wb", h)] = wb_pool.tile([P, K], BF16, name="wb", tag="wb")
+            wb = live[("wb", h)]
             for c in range(pieces):
                 cols = slice(first + c * step, first + (c + 1) * step)
                 nc.vector.tensor_tensor(out=wb[:, cols], in0=w_rows[h][:, cols].bitcast(FP8), in1=scale_rows[:, cols], op=ALU.mult)
-            if first:
-                nc.scalar.copy(out=wb[:, 0:first], in_=w_rows[h][:, 0:first].bitcast(FP8))
+
+        def cast_first(h):
+            live[("wb", h)] = wb_pool.tile([P, K], BF16, name="wb", tag="wb")
+            nc.scalar.copy(out=live[("wb", h)][:, 0:512], in_=w_rows[h][:, 0:512].bitcast(FP8))
 
         def w_turn(h, s):
             if s == 0:
@@ -334,22 +337,21 @@ def tile_attention_pa_kernel(tc, x, w_bytes, w_scale, b, norm_w, out):
         spread_scales()
         for i in range(HEADS):
             product(i)
-            if on(i - LAG_E):
-                squares(i - LAG_E)
             for s in range(2):
                 if on(i - LAG_B):
                     w_turn(i - LAG_B, s)
                 for g in x_turns.get((i, s), ()):
                     x_turn(g, 0)
                     x_turn(g, 1)
+            if on(i - LAG_E):
+                squares(i - LAG_E)
+                table_products(i - LAG_E)
             for g in x_quants_early.get(i, ()):
                 x_quantize(g)
             if on(i - LAG_C):
                 w_quantize(i - LAG_C, 0, 2048)
             for g in x_quants_late.get(i, ()):
                 x_quantize(g)
-            if on(i - LAG_E):
-                table_products(i - LAG_E)
             if on(i - LAG_F):
                 turn_back(i - LAG_F, (0, 1))
                 sums(i - LAG_F, (0, 1))
@@ -369,6 +371,8 @@ def tile_attention_pa_kernel(tc, x, w_bytes, w_scale, b, norm_w, out):
                 w_quantize(i - LAG_C, 2048, 3072)
             if on(i - LAG_F):
                 finish(i - LAG_F)
+            if (i + 1) in SCALAR_HEADS:
+                cast_first(i + 1)
             if i == 1:
                 turn_vectors()
 

@@ -40,9 +40,9 @@ def tile_attention_pa_kernel(tc, x, w_bytes, w_scale, b, norm_w, out):
         code_pool = ctx.enter_context(tc.tile_pool(name="code_pool", bufs=3))
         epi_pool = ctx.enter_context(tc.tile_pool(name="epi_pool", bufs=3))
         res_pool = ctx.enter_context(tc.tile_pool(name="res_pool", bufs=3))
-        psum_tp = ctx.enter_context(tc.psum_pool(name="psum_tp", bufs=4))
+        psum_tp = ctx.enter_context(tc.psum_pool(name="psum_tp", bufs=3))
         psum_z = ctx.enter_context(tc.psum_pool(name="psum_z", bufs=2))
-        psum_rot = ctx.enter_context(tc.psum_pool(name="psum_rot", bufs=1))
+        psum_rot = ctx.enter_context(tc.psum_pool(name="psum_rot", bufs=2))
         psum_ss = ctx.enter_context(tc.psum_pool(name="psum_ss", bufs=1))
         ctx.enter_context(tc.manual_schedule())
 

@@ -354,7 +354,6 @@ def tile_attention_pa_kernel(tc, x, w_bytes, w_scale, b, norm_w, out):
                 x_quantize(g)
             if on(i - LAG_F):
                 turn_back(i - LAG_F, (0, 1))
-                sums(i - LAG_F, (0, 1))
             if on(i - LAG_D):
                 multiply(i - LAG_D, (0, 1, 2))
             if on(i - LAG_B):
@@ -364,7 +363,7 @@ def tile_attention_pa_kernel(tc, x, w_bytes, w_scale, b, norm_w, out):
                 x_turn(g, 1)
             if on(i - LAG_F):
                 turn_back(i - LAG_F, (2, 3))
-                sums(i - LAG_F, (2, 3))
+                sums(i - LAG_F, (0, 1, 2, 3))
             if on(i - LAG_D):
                 multiply(i - LAG_D, (3, 4, 5))
             if on(i - LAG_C):

@@ -353,19 +353,16 @@ def tile_attention_pa_kernel(tc, x, w_bytes, w_scale, b, norm_w, out):
             for g in x_quants_late.get(i, ()):
                 x_quantize(g)
             if on(i - LAG_F):
-                turn_back(i - LAG_F, (0, 1))
-            if on(i - LAG_D):
-                multiply(i - LAG_D, (0, 1, 2))
+                sums(i - LAG_F, (0, 1, 2, 3))
             if on(i - LAG_B):
                 w_turn(i - LAG_B, 2)
             for g in x_turns.get((i, 2), ()):
                 x_turn(g, 0)
                 x_turn(g, 1)
             if on(i - LAG_F):
-                turn_back(i - LAG_F, (2, 3))
-                sums(i - LAG_F, (0, 1, 2, 3))
+                turn_back(i - LAG_F, (0, 1, 2, 3))
             if on(i - LAG_D):
-                multiply(i - LAG_D, (3, 4, 5))
+                multiply(i - LAG_D, (0, 1, 2, 3, 4, 5))
             if on(i - LAG_C):
                 w_quantize(i - LAG_C, 2048, 3072)
             if on(i - LAG_F):

@@ -23,7 +23,9 @@ PI = 3.141592653589793
 ONES_W = 64
 
 LAG_B, LAG_C, LAG_D, LAG_E, LAG_F = 1, 1, 2, 3, 4
-SCALAR_HEADS = tuple(range(1, HEADS, 2))
+G_HEADS = tuple(range(1, HEADS))
+G_FROM = K - 512
+OVERLAP = 16
 
 FLOPS = 2 * TOKENS * K * K
 
@@ -35,6 +37,7 @@ def tile_attention_pa_kernel(tc, x, w_bytes, w_scale, b, norm_w, out):
         byte_pool = ctx.enter_context(tc.tile_pool(name="byte_pool", bufs=HEADS))
         x_pool = ctx.enter_context(tc.tile_pool(name="x_pool", bufs=3))
         xg_pool = ctx.enter_context(tc.tile_pool(name="xg_pool", bufs=4))
+        cast_pool = ctx.enter_context(tc.tile_pool(name="cast_pool", bufs=2))
         wb_pool = ctx.enter_context(tc.tile_pool(name="wb_pool", bufs=3))
         grp_pool = ctx.enter_context(tc.tile_pool(name="grp_pool", bufs=3))
         code_pool = ctx.enter_context(tc.tile_pool(name="code_pool", bufs=3))
@@ -62,8 +65,6 @@ def tile_attention_pa_kernel(tc, x, w_bytes, w_scale, b, norm_w, out):
         scale_view = w_scale.rearrange("o (m q) -> (o m) q", q=P)
         nc.sync.dma_start(out=scale_in[0:HEADS, :], in_=scale_view)
         nc.sync.dma_start(out=scale_in[HEADS:32, :], in_=scale_view[0 : 32 - HEADS, :])
-        scale_first = const.tile([P, 4], F32, name="scale_first")
-        nc.sync.dma_start(out=scale_first[:], in_=w_scale[:, 0:512].rearrange("o (p t) -> p (o t)", t=4))
         w_rows = []
 
         def load_w(h):
@@ -218,18 +219,20 @@ def tile_attention_pa_kernel(tc, x, w_bytes, w_scale, b, norm_w, out):
 
         def product(h):
             pieces = 6 if h == 0 else 1
-            first = 512 if h in SCALAR_HEADS else 0
-            step = (K - first) // pieces
-            if not first:
-                live[("wb", h)] = wb_pool.tile([P, K], BF16, name="wb", tag="wb")
+            live[("wb", h)] = wb_pool.tile([P, K], BF16, name="wb", tag="wb")
             wb = live[("wb", h)]
+            width = G_FROM + OVERLAP if h in G_HEADS else K
+            step = width // pieces
             for c in range(pieces):
-                cols = slice(first + c * step, first + (c + 1) * step)
+                cols = slice(c * step, (c + 1) * step)
                 nc.vector.tensor_tensor(out=wb[:, cols], in0=w_rows[h][:, cols].bitcast(FP8), in1=scale_rows[:, cols], op=ALU.mult)
 
-        def cast_first(h):
-            live[("wb", h)] = wb_pool.tile([P, K], BF16, name="wb", tag="wb")
-            nc.scalar.copy(out=live[("wb", h)][:, 0:512], in_=w_rows[h][:, 0:512].bitcast(FP8))
+        def cast_last(h):
+            live[("cast", h)] = cast_pool.tile([P, K - G_FROM], BF16, name="cast", tag="cast")
+            nc.scalar.copy(out=live[("cast", h)][:], in_=w_rows[h][:, G_FROM:K].bitcast(FP8))
+
+        def product_last(h):
+            nc.gpsimd.tensor_tensor(out=live[("wb", h)][:, G_FROM:K], in0=live[("cast", h)][:], in1=scale_rows[:, G_FROM:K], op=ALU.mult)
 
         def w_turn(h, s):
             if s == 0:
@@ -237,19 +240,6 @@ def tile_attention_pa_kernel(tc, x, w_bytes, w_scale, b, norm_w, out):
             grp_words = live[("grp", h)][:].bitcast(F32).rearrange("p (g r u) -> p g r u", g=PASSES, r=P, u=2)
             words = live[("wb", h)][:].bitcast(F32)
             sources = [[words[:, 256 * (2 * s + a) + u : 256 * (2 * s + a + 1) : 2] for u in range(2)] for a in range(2)]
-            if s == 0 and h in SCALAR_HEADS:
-                tp = psum_tp.tile([P, 2, 2, P], F32, name="tp", tag="tp")
-                for a in range(2):
-                    for u in range(2):
-                        nc.tensor.transpose(tp[:, a, u, :], sources[a][u], ident[:])
-                first = live[("grp", h)][:, 0:512].rearrange("p (r t) -> p r t", t=4)
-                for u in range(2):
-                    halves = tp[:, 0, u, :].bitcast(BF16).rearrange("p (r e) -> p r e", e=2)
-                    for e in range(2):
-                        t = 2 * u + e
-                        nc.scalar.activation(out=first[:, :, t], in_=halves[:, :, e], func=ACT.Copy, scale=scale_first[:, t : t + 1])
-                nc.scalar.copy(out=grp_words[:, 1, :, :], in_=tp[:, 1, :, :].rearrange("p u r -> p r u"))
-                return
             turn(grp_words[:, 2 * s : 2 * s + 2, :, :], sources)
 
         def w_quantize(h, lo, hi):
@@ -337,6 +327,8 @@ def tile_attention_pa_kernel(tc, x, w_bytes, w_scale, b, norm_w, out):
         spread_scales()
         for i in range(HEADS):
             product(i)
+            if i in G_HEADS:
+                product_last(i)
             for s in range(2):
                 if on(i - LAG_B):
                     w_turn(i - LAG_B, s)
@@ -367,8 +359,8 @@ def tile_attention_pa_kernel(tc, x, w_bytes, w_scale, b, norm_w, out):
                 w_quantize(i - LAG_C, 2048, 3072)
             if on(i - LAG_F):
                 finish(i - LAG_F)
-            if (i + 1) in SCALAR_HEADS:
-                cast_first(i + 1)
+            if (i + 1) in G_HEADS:
+                cast_last(i + 1)
             if i == 1:
                 turn_vectors()
 

@@ -23,9 +23,10 @@ PI = 3.141592653589793
 ONES_W = 64
 
 LAG_B, LAG_C, LAG_D, LAG_E, LAG_F = 1, 1, 2, 3, 4
-G_HEADS = tuple(range(1, HEADS))
-G_FROM = K - 512
+G_HEADS = tuple(range(3, HEADS))
+G_FROM = K - 448
 OVERLAP = 16
+V_SPLIT = 1536
 
 FLOPS = 2 * TOKENS * K * K
 
@@ -221,11 +222,15 @@ def tile_attention_pa_kernel(tc, x, w_bytes, w_scale, b, norm_w, out):
             pieces = 6 if h == 0 else 1
             live[("wb", h)] = wb_pool.tile([P, K], BF16, name="wb", tag="wb")
             wb = live[("wb", h)]
-            width = G_FROM + OVERLAP if h in G_HEADS else K
-            step = width // pieces
-            for c in range(pieces):
-                cols = slice(c * step, (c + 1) * step)
+            if h in G_HEADS:
+                spans = [(V_SPLIT, G_FROM + OVERLAP), (0, V_SPLIT)]
+            else:
+                spans = [(c * K // pieces, (c + 1) * K // pieces) for c in range(pieces)]
+            for lo, hi in spans:
+                cols = slice(lo, hi)
                 nc.vector.tensor_tensor(out=wb[:, cols], in0=w_rows[h][:, cols].bitcast(FP8), in1=scale_rows[:, cols], op=ALU.mult)
+                if h in G_HEADS and lo:
+                    product_last(h)
 
         def cast_last(h):
             live[("cast", h)] = cast_pool.tile([P, K - G_FROM], BF16, name="cast", tag="cast")
@@ -327,8 +332,6 @@ def tile_attention_pa_kernel(tc, x, w_bytes, w_scale, b, norm_w, out):
         spread_scales()
         for i in range(HEADS):
             product(i)
-            if i in G_HEADS:
-                product_last(i)
             for s in range(2):
                 if on(i - LAG_B):
                     w_turn(i - LAG_B, s)

@@ -24,9 +24,12 @@ ONES_W = 64
 
 LAG_B, LAG_C, LAG_D, LAG_E, LAG_F = 1, 1, 2, 3, 4
 G_HEADS = tuple(range(3, HEADS))
-G_FROM = K - 448
+G_FROM = K - 640
+G_TURN = K - 512
 OVERLAP = 16
-V_SPLIT = 1536
+V_SPLIT = 1728
+E_PASSES = 2
+E_TO = 1024
 
 FLOPS = 2 * TOKENS * K * K
 
@@ -66,6 +69,7 @@ def tile_attention_pa_kernel(tc, x, w_bytes, w_scale, b, norm_w, out):
         scale_view = w_scale.rearrange("o (m q) -> (o m) q", q=P)
         nc.sync.dma_start(out=scale_in[0:HEADS, :], in_=scale_view)
         nc.sync.dma_start(out=scale_in[HEADS:32, :], in_=scale_view[0 : 32 - HEADS, :])
+        scale_kt = const.tile([P, E_PASSES, 4], F32, name="scale_kt")
         w_rows = []
 
         def load_w(h):
@@ -86,6 +90,7 @@ def tile_attention_pa_kernel(tc, x, w_bytes, w_scale, b, norm_w, out):
         load_w(1)
         nc.sync.dma_start(out=vec_rows[0:HEADS, :], in_=b.rearrange("(h d) -> h d", d=P))
         nc.sync.dma_start(out=vec_rows[HEADS : HEADS + 1, :], in_=norm_w.rearrange("(o d) -> o d", o=1))
+        nc.sync.dma_start(out=scale_kt[:], in_=w_scale[:, 0:E_TO].rearrange("o (g p t) -> p (o g) t", p=P, t=4))
         load_x(1)
         load_x(2)
         for h in range(2, HEADS):
@@ -140,11 +145,14 @@ def tile_attention_pa_kernel(tc, x, w_bytes, w_scale, b, norm_w, out):
         tables = const.tile([P, 2, TOKENS], F32, name="tables")
         raw_tables = const.tile([P, 2, TOKENS], F32, name="raw_tables")
 
-        def spread_scales():
+        def turn_scales():
             turned = psum_tp.tile([P, P], F32, name="turned", tag="tp")
             nc.tensor.transpose(turned[:], scale_in[:], ident[:])
             scale_cols = const.tile([P, HEADS], F32, name="scale_cols")
-            nc.scalar.copy(out=scale_cols[:], in_=turned[:, 0:HEADS])
+            nc.vector.tensor_copy(out=scale_cols[:], in_=turned[:, 0:HEADS])
+            return scale_cols
+
+        def spread_scales(scale_cols):
             for c in range(PASSES):
                 spread = psum_tp.tile([P, 4, P], F32, name="spread", tag="tp")
                 for a in range(4):
@@ -220,32 +228,64 @@ def tile_attention_pa_kernel(tc, x, w_bytes, w_scale, b, norm_w, out):
 
         def product(h):
             pieces = 6 if h == 0 else 1
-            live[("wb", h)] = wb_pool.tile([P, K], BF16, name="wb", tag="wb")
+            if h not in G_HEADS:
+                live[("wb", h)] = wb_pool.tile([P, K], BF16, name="wb", tag="wb")
             wb = live[("wb", h)]
             if h in G_HEADS:
-                spans = [(V_SPLIT, G_FROM + OVERLAP), (0, V_SPLIT)]
+                spans = [(V_SPLIT, G_FROM + OVERLAP), (E_TO, V_SPLIT)]
             else:
                 spans = [(c * K // pieces, (c + 1) * K // pieces) for c in range(pieces)]
             for lo, hi in spans:
                 cols = slice(lo, hi)
                 nc.vector.tensor_tensor(out=wb[:, cols], in0=w_rows[h][:, cols].bitcast(FP8), in1=scale_rows[:, cols], op=ALU.mult)
-                if h in G_HEADS and lo:
-                    product_last(h)
+            if h in G_HEADS:
+                product_last(h)
 
         def cast_last(h):
+            live[("wb", h)] = wb_pool.tile([P, K], BF16, name="wb", tag="wb")
+            nc.scalar.copy(out=live[("wb", h)][:, 0:E_TO], in_=w_rows[h][:, 0:E_TO].bitcast(FP8))
             live[("cast", h)] = cast_pool.tile([P, K - G_FROM], BF16, name="cast", tag="cast")
             nc.scalar.copy(out=live[("cast", h)][:], in_=w_rows[h][:, G_FROM:K].bitcast(FP8))
 
         def product_last(h):
-            nc.gpsimd.tensor_tensor(out=live[("wb", h)][:, G_FROM:K], in0=live[("cast", h)][:], in1=scale_rows[:, G_FROM:K], op=ALU.mult)
+            nc.gpsimd.tensor_tensor(
+                out=live[("wb", h)][:, G_FROM:G_TURN], in0=live[("cast", h)][:, 0 : G_TURN - G_FROM], in1=scale_rows[:, G_FROM:G_TURN], op=ALU.mult
+            )
+            nc.gpsimd.tensor_tensor(
+                out=live[("wb", h)][:, G_TURN:K].rearrange("p (u c e) -> p u c e", u=2, e=2),
+                in0=live[("cast", h)][:, G_TURN - G_FROM :].rearrange("p (c u e) -> p u c e", u=2, e=2),
+                in1=scale_rows[:, G_TURN:K].rearrange("p (c u e) -> p u c e", u=2, e=2),
+                op=ALU.mult,
+            )
 
         def w_turn(h, s):
+            if s == 0 and h in G_HEADS:
+                return
             if s == 0:
                 live[("grp", h)] = grp_pool.tile([P, K], BF16, name="grp", tag="grp", align_bytes=64)
             grp_words = live[("grp", h)][:].bitcast(F32).rearrange("p (g r u) -> p g r u", g=PASSES, r=P, u=2)
             words = live[("wb", h)][:].bitcast(F32)
             sources = [[words[:, 256 * (2 * s + a) + u : 256 * (2 * s + a + 1) : 2] for u in range(2)] for a in range(2)]
+            if s == 2 and h in G_HEADS:
+                sources[1] = [words[:, 1280 + P * u : 1280 + P * (u + 1)] for u in range(2)]
             turn(grp_words[:, 2 * s : 2 * s + 2, :, :], sources)
+
+        def early_turn(h):
+            live[("grp", h)] = grp_pool.tile([P, K], BF16, name="grp", tag="grp", align_bytes=64)
+            words = live[("wb", h)][:].bitcast(F32)
+            tp = psum_tp.tile([P, 2, E_PASSES, P], F32, name="tp", tag="tp")
+            live[("etp", h)] = tp
+            for a in range(E_PASSES):
+                for u in range(2):
+                    nc.tensor.transpose(tp[:, u, a, :], words[:, 256 * a + u : 256 * (a + 1) : 2], ident[:])
+
+        def early_product(h):
+            nc.vector.tensor_tensor(
+                out=live[("grp", h)][:, 0:E_TO].rearrange("p (a r u e) -> p a r u e", a=E_PASSES, u=2, e=2),
+                in0=live[("etp", h)][:].bitcast(BF16).rearrange("p u a (r e) -> p a r u e", e=2),
+                in1=scale_kt[:].rearrange("p a (u e) -> p a u e", u=2).unsqueeze(2).to_broadcast([P, E_PASSES, P, 2, 2]),
+                op=ALU.mult,
+            )
 
         def w_quantize(h, lo, hi):
             if lo == 0:
@@ -326,10 +366,11 @@ def tile_attention_pa_kernel(tc, x, w_bytes, w_scale, b, norm_w, out):
         x_quants_early = {1: (0, 1), 2: (2, 3)}
         x_quants_late = {2: (4, 5)}
 
+        scale_cols = turn_scales()
         folded_angles = angles()
         nc.scalar.activation(out=sin_cos[:], in_=folded_angles[:], func=ACT.Sin)
         build_tables()
-        spread_scales()
+        spread_scales(scale_cols)
         for i in range(HEADS):
             product(i)
             for s in range(2):
@@ -341,12 +382,6 @@ def tile_attention_pa_kernel(tc, x, w_bytes, w_scale, b, norm_w, out):
             if on(i - LAG_E):
                 squares(i - LAG_E)
                 table_products(i - LAG_E)
-            for g in x_quants_early.get(i, ()):
-                x_quantize(g)
-            if on(i - LAG_C):
-                w_quantize(i - LAG_C, 0, 2048)
-            for g in x_quants_late.get(i, ()):
-                x_quantize(g)
             if on(i - LAG_F):
                 sums(i - LAG_F, (0, 1, 2, 3))
             if on(i - LAG_B):
@@ -356,6 +391,15 @@ def tile_attention_pa_kernel(tc, x, w_bytes, w_scale, b, norm_w, out):
                 x_turn(g, 1)
             if on(i - LAG_F):
                 turn_back(i - LAG_F, (0, 1, 2, 3))
+            if i in G_HEADS:
+                early_turn(i)
+                early_product(i)
+            for g in x_quants_early.get(i, ()):
+                x_quantize(g)
+            if on(i - LAG_C):
+                w_quantize(i - LAG_C, 0, 2048)
+            for g in x_quants_late.get(i, ()):
+                x_quantize(g)
             if on(i - LAG_D):
                 multiply(i - LAG_D, (0, 1, 2, 3, 4, 5))
             if on(i - LAG_C):

@@ -383,14 +383,13 @@ def tile_attention_pa_kernel(tc, x, w_bytes, w_scale, b, norm_w, out):
                 squares(i - LAG_E)
                 table_products(i - LAG_E)
             if on(i - LAG_F):
+                turn_back(i - LAG_F, (0, 1, 2, 3))
                 sums(i - LAG_F, (0, 1, 2, 3))
             if on(i - LAG_B):
                 w_turn(i - LAG_B, 2)
             for g in x_turns.get((i, 2), ()):
                 x_turn(g, 0)
                 x_turn(g, 1)
-            if on(i - LAG_F):
-                turn_back(i - LAG_F, (0, 1, 2, 3))
             if i in G_HEADS:
                 early_turn(i)
                 early_product(i)

from contextlib import ExitStack

import concourse.mybir as mybir
from concourse.masks import make_identity

F32 = mybir.dt.float32
BF16 = mybir.dt.bfloat16
I32 = mybir.dt.int32
U32 = mybir.dt.uint32
U8 = mybir.dt.uint8
FP8 = mybir.dt.float8_e4m3fn
FP8X4 = mybir.dt.float8_e4m3fn_x4
ALU = mybir.AluOpType
ACT = mybir.ActivationFunctionType

P = 128
TOKENS = 512
K = 3072
HEADS = 24
PASSES = K // 512
EPS = 1e-6
PI = 3.141592653589793
ONES_W = 64

LAG_B, LAG_C, LAG_D, LAG_E, LAG_F = 1, 1, 2, 3, 4
G_HEADS = tuple(range(3, HEADS))
G_FROM = K - 640
G_TURN = K - 512
OVERLAP = 16
V_SPLIT = 1728
E_PASSES = 2
E_TO = 1024

FLOPS = 2 * TOKENS * K * K


def tile_attention_pa_kernel(tc, x, w_bytes, w_scale, b, norm_w, out):
    nc = tc.nc
    with ExitStack() as ctx:
        const = ctx.enter_context(tc.tile_pool(name="const", bufs=1))
        byte_pool = ctx.enter_context(tc.tile_pool(name="byte_pool", bufs=HEADS))
        x_pool = ctx.enter_context(tc.tile_pool(name="x_pool", bufs=3))
        xg_pool = ctx.enter_context(tc.tile_pool(name="xg_pool", bufs=4))
        cast_pool = ctx.enter_context(tc.tile_pool(name="cast_pool", bufs=2))
        wb_pool = ctx.enter_context(tc.tile_pool(name="wb_pool", bufs=3))
        grp_pool = ctx.enter_context(tc.tile_pool(name="grp_pool", bufs=3))
        code_pool = ctx.enter_context(tc.tile_pool(name="code_pool", bufs=3))
        epi_pool = ctx.enter_context(tc.tile_pool(name="epi_pool", bufs=3))
        res_pool = ctx.enter_context(tc.tile_pool(name="res_pool", bufs=3))
        psum_tp = ctx.enter_context(tc.psum_pool(name="psum_tp", bufs=3))
        psum_z = ctx.enter_context(tc.psum_pool(name="psum_z", bufs=2))
        psum_rot = ctx.enter_context(tc.psum_pool(name="psum_rot", bufs=2))
        psum_ss = ctx.enter_context(tc.psum_pool(name="psum_ss", bufs=1))
        ctx.enter_context(tc.manual_schedule())

        d_int = const.tile([P, 1], I32, name="d_int")
        nc.gpsimd.iota(d_int[:], pattern=[[0, 1]], base=0, channel_multiplier=1)
        col_idx = const.tile([P, P], F32, name="col_idx")
        nc.gpsimd.iota(col_idx[:], pattern=[[1, P]], base=0, channel_multiplier=0, allow_small_or_imprecise_dtypes=True)
        scale_in = const.tile([P, P], F32, name="scale_in")
        nc.vector.memset(scale_in[32:64, :], 0.0)
        nc.vector.memset(scale_in[64:128, :], 0.0)
        base_col = const.tile([P, 1], F32, name="base_col")
        nc.vector.memset(base_col[:], 10000.0)
        vec_rows = const.tile([P, P], BF16, name="vec_rows")
        nc.vector.memset(vec_rows[:], 0.0)
        ident = const.tile([P, P], F32, name="ident")

        scale_view = w_scale.rearrange("o (m q) -> (o m) q", q=P)
        nc.sync.dma_start(out=scale_in[0:HEADS, :], in_=scale_view)
        nc.sync.dma_start(out=scale_in[HEADS:32, :], in_=scale_view[0 : 32 - HEADS, :])
        scale_kt = const.tile([P, E_PASSES, 4], F32, name="scale_kt")
        w_rows = []

        def load_w(h):
            t = byte_pool.tile([P, K], U8, name="w_code_bytes", tag="w_code_bytes")
            nc.sync.dma_start(out=t[:], in_=w_bytes[h * P : (h + 1) * P, :])
            w_rows.append(t)

        x_view = x[0].rearrange("(j p) k -> p j k", p=P)
        x_parts = []

        def load_x(c):
            t = x_pool.tile([P, 4, 1024], BF16, name="x_part", tag="x_part")
            nc.sync.dma_start(out=t[:], in_=x_view[:, :, c * 1024 : (c + 1) * 1024])
            x_parts.append(t)

        load_w(0)
        load_x(0)
        load_w(1)
        nc.sync.dma_start(out=vec_rows[0:HEADS, :], in_=b.rearrange("(h d) -> h d", d=P))
        nc.sync.dma_start(out=vec_rows[HEADS : HEADS + 1, :], in_=norm_w.rearrange("(o d) -> o d", o=1))
        nc.sync.dma_start(out=scale_kt[:], in_=w_scale[:, 0:E_TO].rearrange("o (g p t) -> p (o g) t", p=P, t=4))
        load_x(1)
        load_x(2)
        for h in range(2, HEADS):
            load_w(h)

        scale_rows = const.tile([P, K], F32, name="scale_rows")
        odd_int = const.tile([P, 1], I32, name="odd_int")
        nc.vector.tensor_scalar(out=odd_int[:], in0=d_int[:], scalar1=1, scalar2=None, op0=ALU.bitwise_and)
        d_col = const.tile([P, 1], F32, name="d_col")
        nc.vector.tensor_copy(out=d_col[:], in_=d_int[:])
        odd = const.tile([P, 1], F32, name="odd")
        nc.vector.tensor_copy(out=odd[:], in_=odd_int[:])
        is_h = const.tile([P, 1], F32, name="is_h")
        nc.vector.tensor_scalar(out=is_h[:], in0=d_col[:], scalar1=44.0, scalar2=None, op0=ALU.is_ge)
        is_w = const.tile([P, 1], F32, name="is_w")
        nc.vector.tensor_scalar(out=is_w[:], in0=d_col[:], scalar1=86.0, scalar2=None, op0=ALU.is_ge)
        even_d = const.tile([P, 1], F32, name="even_d")
        nc.vector.tensor_tensor(out=even_d[:], in0=d_col[:], in1=odd[:], op=ALU.subtract)
        m2a = const.tile([P, 1], F32, name="m2a")
        nc.vector.scalar_tensor_tensor(out=m2a[:], in0=is_h[:], scalar=-44.0, in1=even_d[:], op0=ALU.mult, op1=ALU.add)
        m2 = const.tile([P, 1], F32, name="m2")
        nc.vector.scalar_tensor_tensor(out=m2[:], in0=is_w[:], scalar=-42.0, in1=m2a[:], op0=ALU.mult, op1=ALU.add)
        neg_inv_dim = const.tile([P, 1], F32, name="neg_inv_dim")
        nc.vector.tensor_scalar(out=neg_inv_dim[:], in0=is_h[:], scalar1=1.0 / 44.0 - 1.0 / 42.0, scalar2=-1.0 / 44.0, op0=ALU.mult, op1=ALU.add)
        expo = const.tile([P, 1], F32, name="expo")
        nc.vector.tensor_tensor(out=expo[:], in0=m2[:], in1=neg_inv_dim[:], op=ALU.mult)
        freq = const.tile([P, 1], F32, name="freq")
        nc.gpsimd.tensor_tensor(out=freq[:], in0=base_col[:], in1=expo[:], op=ALU.pow)
        nc.vector.tensor_scalar(out=ident[:], in0=col_idx[:], scalar1=d_col[:, 0:1], scalar2=None, op0=ALU.is_equal)
        sign = const.tile([P, 1], F32, name="sign")
        nc.vector.tensor_scalar(out=sign[:], in0=odd[:], scalar1=-2.0, scalar2=1.0, op0=ALU.mult, op1=ALU.add)
        mask_t = const.tile([P, 1], F32, name="mask_t")
        nc.vector.tensor_scalar(out=mask_t[:], in0=is_h[:], scalar1=-1.0, scalar2=1.0, op0=ALU.mult, op1=ALU.add)
        mask_h = const.tile([P, 1], F32, name="mask_h")
        nc.vector.tensor_tensor(out=mask_h[:], in0=is_h[:], in1=is_w[:], op=ALU.subtract)

        ident_bf = const.tile([P, P], BF16, name="ident_bf")
        make_identity(nc, ident_bf[:])
        swap = const.tile([P, P], F32, name="swap")
        ident_pairs = ident[:].rearrange("p (m e) -> p m e", e=2)
        swap_pairs = swap[:].rearrange("p (m e) -> p m e", e=2)
        nc.gpsimd.tensor_copy(out=swap_pairs[:, :, 0], in_=ident_pairs[:, :, 1])
        nc.gpsimd.tensor_copy(out=swap_pairs[:, :, 1], in_=ident_pairs[:, :, 0])
        ones = const.tile([P, ONES_W], F32, name="ones")
        nc.gpsimd.memset(ones[:], 1.0)
        eps_col = const.tile([P, 1], F32, name="eps_col")
        nc.gpsimd.memset(eps_col[:], EPS)

        sin_cos = const.tile([P, 16], F32, name="sin_cos")
        vec_cols = const.tile([P, 32], F32, name="vec_cols")
        vec_scaled = const.tile([P, 32], F32, name="vec_scaled")
        tables = const.tile([P, 2, TOKENS], F32, name="tables")
        raw_tables = const.tile([P, 2, TOKENS], F32, name="raw_tables")

        def turn_scales():
            turned = psum_tp.tile([P, P], F32, name="turned", tag="tp")
            nc.tensor.transpose(turned[:], scale_in[:], ident[:])
            scale_cols = const.tile([P, HEADS], F32, name="scale_cols")
            nc.vector.tensor_copy(out=scale_cols[:], in_=turned[:, 0:HEADS])
            return scale_cols

        def spread_scales(scale_cols):
            for c in range(PASSES):
                spread = psum_tp.tile([P, 4, P], F32, name="spread", tag="tp")
                for a in range(4):
                    m = 4 * c + a
                    nc.tensor.transpose(spread[:, a, :], scale_cols[:, m : m + 1].to_broadcast([P, P]), ident[:])
                nc.scalar.copy(out=scale_rows[:, c * 512 : (c + 1) * 512], in_=spread[:].rearrange("p a q -> p (a q)"))

        def angles():
            angle = const.tile([P, 16], F32, name="angle")
            nc.vector.tensor_scalar(out=angle[:, 0:8], in0=col_idx[:, 0:8], scalar1=freq[:, 0:1], scalar2=PI / 2.0, op0=ALU.mult, op1=ALU.add)
            nc.vector.tensor_scalar(out=angle[:, 8:16], in0=col_idx[:, 0:8], scalar1=freq[:, 0:1], scalar2=None, op0=ALU.mult)
            wrap = const.tile([P, 16], F32, name="wrap")
            nc.vector.tensor_scalar(out=wrap[:], in0=angle[:], scalar1=PI, scalar2=-2.0 * PI, op0=ALU.is_gt, op1=ALU.mult)
            folded = const.tile([P, 16], F32, name="folded")
            nc.vector.tensor_tensor(out=folded[:], in0=angle[:], in1=wrap[:], op=ALU.add)
            nc.vector.tensor_scalar(out=folded[:, 8:16], in0=folded[:, 8:16], scalar1=sign[:, 0:1], scalar2=None, op0=ALU.mult)
            return folded

        small_tabs = {}

        def turn_vectors():
            vec_ps = psum_tp.tile([P, P], BF16, name="vec_ps", tag="tp")
            nc.tensor.transpose(vec_ps[:], vec_rows[:], ident_bf[:])
            nc.scalar.copy(out=vec_cols[:], in_=vec_ps[:, 0:32])
            nc.scalar.activation(out=vec_scaled[:], in_=vec_cols[:], func=ACT.Copy, scale=float(P) ** -0.5)
            gain = vec_cols[:, HEADS : HEADS + 1]
            nc.scalar.activation(
                out=tables[:].rearrange("p w n -> p (w n)"), in_=raw_tables[:].rearrange("p w n -> p (w n)"), func=ACT.Copy, scale=gain
            )

        def build_tables():
            for name, mask in (("t", mask_t), ("h", mask_h), ("w", is_w)):
                masked = const.tile([P, 2, 8], F32, name="tab_" + name)
                nc.vector.tensor_scalar(out=masked[:].rearrange("p w v -> p (w v)"), in0=sin_cos[:], scalar1=mask[:, 0:1], scalar2=None, op0=ALU.mult)
                small_tabs[name] = masked
            by_ij = const.tile([P, 2, 64], F32, name="by_ij")
            nc.vector.tensor_tensor(
                out=by_ij[:].rearrange("p w (i j) -> p w i j", i=8),
                in0=small_tabs["h"][:].unsqueeze(3).to_broadcast([P, 2, 8, 8]),
                in1=small_tabs["w"][:].unsqueeze(2).to_broadcast([P, 2, 8, 8]),
                op=ALU.add,
            )
            nc.vector.tensor_tensor(
                out=raw_tables[:].rearrange("p w (t r) -> p w t r", t=8),
                in0=small_tabs["t"][:].unsqueeze(3).to_broadcast([P, 2, 8, 64]),
                in1=by_ij[:].unsqueeze(2).to_broadcast([P, 2, 8, 64]),
                op=ALU.add,
            )

        x_codes = const.tile([P, PASSES * TOKENS], U32, name="x_codes", align_bytes=64)
        x_scales = const.tile([P, PASSES * TOKENS], U8, name="x_scales", align_bytes=64)
        live = {}

        def turn(dst_words, sources):
            tp = psum_tp.tile([P, 2, 2, P], F32, name="tp", tag="tp")
            for a in range(2):
                for u in range(2):
                    nc.tensor.transpose(tp[:, a, u, :], sources[a][u], ident[:])
            nc.scalar.copy(out=dst_words, in_=tp[:].rearrange("p a u r -> p a r u"))

        def x_turn(g, jp):
            if jp == 0:
                live[("xg", g)] = xg_pool.tile([P, 2048], BF16, name="xg", tag="xg", align_bytes=64)
            lo = 256 * (g % 2)
            turn(
                live[("xg", g)][:, jp * 1024 : (jp + 1) * 1024].bitcast(F32).rearrange("p (a r u) -> p a r u", a=2, r=P, u=2),
                [[x_parts[g // 2][:, 2 * jp + a, :].bitcast(F32)[:, lo + u : lo + 256 : 2] for u in range(2)] for a in range(2)],
            )

        def x_quantize(g):
            cols = slice(g * TOKENS, (g + 1) * TOKENS)
            nc.vector.quantize_mx(out=x_codes[:, cols].bitcast(FP8X4), scales=x_scales[:, cols], in_=live[("xg", g)][:])

        def product(h):
            pieces = 6 if h == 0 else 1
            if h not in G_HEADS:
                live[("wb", h)] = wb_pool.tile([P, K], BF16, name="wb", tag="wb")
            wb = live[("wb", h)]
            if h in G_HEADS:
                spans = [(V_SPLIT, G_FROM + OVERLAP), (E_TO, V_SPLIT)]
            else:
                spans = [(c * K // pieces, (c + 1) * K // pieces) for c in range(pieces)]
            for lo, hi in spans:
                cols = slice(lo, hi)
                nc.vector.tensor_tensor(out=wb[:, cols], in0=w_rows[h][:, cols].bitcast(FP8), in1=scale_rows[:, cols], op=ALU.mult)
            if h in G_HEADS:
                product_last(h)

        def cast_last(h):
            live[("wb", h)] = wb_pool.tile([P, K], BF16, name="wb", tag="wb")
            nc.scalar.copy(out=live[("wb", h)][:, 0:E_TO], in_=w_rows[h][:, 0:E_TO].bitcast(FP8))
            live[("cast", h)] = cast_pool.tile([P, K - G_FROM], BF16, name="cast", tag="cast")
            nc.scalar.copy(out=live[("cast", h)][:], in_=w_rows[h][:, G_FROM:K].bitcast(FP8))

        def product_last(h):
            nc.gpsimd.tensor_tensor(
                out=live[("wb", h)][:, G_FROM:G_TURN], in0=live[("cast", h)][:, 0 : G_TURN - G_FROM], in1=scale_rows[:, G_FROM:G_TURN], op=ALU.mult
            )
            nc.gpsimd.tensor_tensor(
                out=live[("wb", h)][:, G_TURN:K].rearrange("p (u c e) -> p u c e", u=2, e=2),
                in0=live[("cast", h)][:, G_TURN - G_FROM :].rearrange("p (c u e) -> p u c e", u=2, e=2),
                in1=scale_rows[:, G_TURN:K].rearrange("p (c u e) -> p u c e", u=2, e=2),
                op=ALU.mult,
            )

        def w_turn(h, s):
            if s == 0 and h in G_HEADS:
                return
            if s == 0:
                live[("grp", h)] = grp_pool.tile([P, K], BF16, name="grp", tag="grp", align_bytes=64)
            grp_words = live[("grp", h)][:].bitcast(F32).rearrange("p (g r u) -> p g r u", g=PASSES, r=P, u=2)
            words = live[("wb", h)][:].bitcast(F32)
            sources = [[words[:, 256 * (2 * s + a) + u : 256 * (2 * s + a + 1) : 2] for u in range(2)] for a in range(2)]
            if s == 2 and h in G_HEADS:
                sources[1] = [words[:, 1280 + P * u : 1280 + P * (u + 1)] for u in range(2)]
            turn(grp_words[:, 2 * s : 2 * s + 2, :, :], sources)

        def early_turn(h):
            live[("grp", h)] = grp_pool.tile([P, K], BF16, name="grp", tag="grp", align_bytes=64)
            words = live[("wb", h)][:].bitcast(F32)
            tp = psum_tp.tile([P, 2, E_PASSES, P], F32, name="tp", tag="tp")
            live[("etp", h)] = tp
            for a in range(E_PASSES):
                for u in range(2):
                    nc.tensor.transpose(tp[:, u, a, :], words[:, 256 * a + u : 256 * (a + 1) : 2], ident[:])

        def early_product(h):
            nc.vector.tensor_tensor(
                out=live[("grp", h)][:, 0:E_TO].rearrange("p (a r u e) -> p a r u e", a=E_PASSES, u=2, e=2),
                in0=live[("etp", h)][:].bitcast(BF16).rearrange("p u a (r e) -> p a r u e", e=2),
                in1=scale_kt[:].rearrange("p a (u e) -> p a u e", u=2).unsqueeze(2).to_broadcast([P, E_PASSES, P, 2, 2]),
                op=ALU.mult,
            )

        def w_quantize(h, lo, hi):
            if lo == 0:
                live[("wc", h)] = code_pool.tile([P, PASSES * P], U32, name="w_codes", tag="w_codes", align_bytes=64)
                live[("ws", h)] = code_pool.tile([P, PASSES * P], U8, name="w_scales", tag="w_scales", align_bytes=64)
            nc.vector.quantize_mx(
                out=live[("wc", h)][:, lo // 4 : hi // 4].bitcast(FP8X4),
                scales=live[("ws", h)][:, lo // 4 : hi // 4],
                in_=live[("grp", h)][:, lo:hi],
            )

        def multiply(h, passes):
            if passes[0] == 0:
                live[("z", h)] = psum_z.tile([P, TOKENS], F32, name="z", tag="z")
            for g in passes:
                nc.tensor.matmul_mx(
                    out=live[("z", h)][:],
                    lhsT=live[("wc", h)][:, g * P : (g + 1) * P].bitcast(FP8X4),
                    lhsT_scale=live[("ws", h)][:, g * P : (g + 1) * P],
                    rhs=x_codes[:, g * TOKENS : (g + 1) * TOKENS].bitcast(FP8X4),
                    rhs_scale=x_scales[:, g * TOKENS : (g + 1) * TOKENS],
                    start=(g == 0),
                    stop=(g == PASSES - 1),
                )

        def squares(h):
            sq = epi_pool.tile([P, TOKENS], F32, name="sq", tag="sq")
            live[("sq", h)] = sq
            nc.scalar.activation(out=sq[:], in_=live[("z", h)][:], func=ACT.Square, bias=vec_scaled[:, h : h + 1], scale=float(P) ** -0.5)

        def table_products(h):
            prod = epi_pool.tile([P, 2, TOKENS], F32, name="prod", tag="prod")
            live[("prod", h)] = prod
            pieces = 2 if h == HEADS - 1 else 1
            step = TOKENS // pieces
            for c in range(pieces):
                cols = slice(c * step, (c + 1) * step)
                nc.vector.scalar_tensor_tensor(
                    out=prod[:, :, cols],
                    in0=live[("z", h)][:, cols].unsqueeze(1).to_broadcast([P, 2, step]),
                    scalar=vec_cols[:, h : h + 1],
                    in1=tables[:, :, cols],
                    op0=ALU.add,
                    op1=ALU.mult,
                )

        def sums(h, tiles):
            if tiles[0] == 0:
                live[("ss", h)] = psum_ss.tile([P, 4, ONES_W], F32, name="ss", tag="ss")
            for j in tiles:
                nc.tensor.matmul(live[("ss", h)][:, j, :], lhsT=live[("sq", h)][:, j * P : (j + 1) * P], rhs=ones[:], start=True, stop=True)

        def turn_back(h, tiles):
            if tiles[0] == 0:
                live[("rot", h)] = psum_rot.tile([P, 4, P], F32, name="rot", tag="rot")
            rot = live[("rot", h)]
            for j in tiles:
                cols = slice(j * P, (j + 1) * P)
                nc.tensor.matmul(rot[:, j, :], lhsT=live[("prod", h)][:, 0, cols], rhs=ident[:], is_transpose=True, start=True, stop=False)
                nc.tensor.matmul(rot[:, j, :], lhsT=live[("prod", h)][:, 1, cols], rhs=swap[:], is_transpose=True, start=False, stop=True)

        def finish(h):
            rstd = res_pool.tile([P, 4], F32, name="rstd", tag="rstd")
            nc.scalar.activation(out=rstd[:], in_=live[("ss", h)][:, :, 0], func=ACT.Abs_reciprocal_sqrt, bias=eps_col[:, 0:1], scale=1.0)
            res = res_pool.tile([P, 4, P], F32, name="res", tag="res")
            out_view = out[0, h].rearrange("(j p) d -> p j d", p=P)
            pieces = 2 if h == HEADS - 1 else 1
            step = 4 // pieces
            for c in range(pieces):
                for j in range(c * step, (c + 1) * step):
                    nc.scalar.activation(out=res[:, j, :], in_=live[("rot", h)][:, j, :], func=ACT.Copy, scale=rstd[:, j : j + 1])
                nc.sync.dma_start(out=out_view[:, c * step : (c + 1) * step, :], in_=res[:, c * step : (c + 1) * step, :])

        def on(h):
            return 0 <= h < HEADS

        x_turns = {(0, 0): (0,), (0, 1): (1,), (1, 2): (2, 3), (2, 0): (4,), (2, 1): (5,)}
        x_quants_early = {1: (0, 1), 2: (2, 3)}
        x_quants_late = {2: (4, 5)}

        scale_cols = turn_scales()
        folded_angles = angles()
        nc.scalar.activation(out=sin_cos[:], in_=folded_angles[:], func=ACT.Sin)
        build_tables()
        spread_scales(scale_cols)
        for i in range(HEADS):
            product(i)
            for s in range(2):
                if on(i - LAG_B):
                    w_turn(i - LAG_B, s)
                for g in x_turns.get((i, s), ()):
                    x_turn(g, 0)
                    x_turn(g, 1)
            if on(i - LAG_E):
                squares(i - LAG_E)
                table_products(i - LAG_E)
            if on(i - LAG_F):
                turn_back(i - LAG_F, (0, 1, 2, 3))
                sums(i - LAG_F, (0, 1, 2, 3))
            if on(i - LAG_B):
                w_turn(i - LAG_B, 2)
            for g in x_turns.get((i, 2), ()):
                x_turn(g, 0)
                x_turn(g, 1)
            if i in G_HEADS:
                early_turn(i)
                early_product(i)
            for g in x_quants_early.get(i, ()):
                x_quantize(g)
            if on(i - LAG_C):
                w_quantize(i - LAG_C, 0, 2048)
            for g in x_quants_late.get(i, ()):
                x_quantize(g)
            if on(i - LAG_D):
                multiply(i - LAG_D, (0, 1, 2, 3, 4, 5))
            if on(i - LAG_C):
                w_quantize(i - LAG_C, 2048, 3072)
            if on(i - LAG_F):
                finish(i - LAG_F)
            if (i + 1) in G_HEADS:
                cast_last(i + 1)
            if i == 1:
                turn_vectors()

        last = HEADS - 1
        squares(last - 2)
        table_products(last - 2)
        for s in range(3):
            w_turn(last, s)
        w_quantize(last, 0, 2048)
        w_quantize(last, 2048, 3072)
        for h in (last - 1, last):
            sums(h - 2, (0, 1, 2, 3))
            turn_back(h - 2, (0, 1, 2, 3))
            finish(h - 2)
            multiply(h, (0, 1, 2, 3, 4, 5))
            squares(h)
            table_products(h)
        for h in (last - 1, last):
            sums(h, (0, 1, 2, 3))
            turn_back(h, (0, 1, 2, 3))
            finish(h)
